import numpy as np
import ml_dtypes


def mxq(x, axis, fmt="e4m3"):
    dtype, down = {"e4m3": (ml_dtypes.float8_e4m3fn, 7), "e5m2": (ml_dtypes.float8_e5m2, 14)}[fmt]
    v = np.moveaxis(np.asarray(x, np.float32).astype(ml_dtypes.bfloat16).astype(np.float64), axis, -1)
    blocks = v.reshape(v.shape[:-1] + (-1, 32))
    amax = np.abs(blocks).max(-1, keepdims=True)
    byte = np.maximum(np.where(amax > 0, np.frexp(amax)[1] - 1 + 127, 0) - down, 1)
    scale = np.exp2(byte - 127.0)
    codes = (blocks / scale).astype(np.float32).astype(dtype).astype(np.float64)
    return np.moveaxis((codes * scale).reshape(v.shape), -1, axis)


WIDE = False


def mx_kscale(k):
    if not WIDE:
        return np.ones(k)
    levels = np.array([10, -10, 5, -5, 0])
    a = np.random.permutation(np.resize(levels, k // 512 * 4)).reshape(k // 512, 4)
    idx = np.arange(k)
    return np.exp2(a[idx // 512, idx % 128 // 32])


BF16 = ml_dtypes.bfloat16


def bf(x):
    return np.asarray(x, np.float32).astype(BF16)


def f64(x):
    return np.asarray(x).astype(np.float64)


B, HC, WC, C, F = 1024, 2, 2, 1024, 256


def setup_inputs():
    s = mx_kscale(C)
    x_crop = np.stack([np.random.standard_normal((B, HC, WC, C)), np.random.standard_normal((B, HC, WC, C))], axis=1)
    return {"x_crop": bf(x_crop * s),
            "W_r": bf(np.random.standard_normal((HC, WC, C, F)) * 0.5 / np.sqrt(C) / s[:, None]),
            "W_i": bf(np.random.standard_normal((HC, WC, C, F)) * 0.5 / np.sqrt(C) / s[:, None]),
            "b_r": bf(np.random.standard_normal(F) * 0.3),
            "b_i": bf(np.random.standard_normal(F) * 0.3)}


def reference(x_crop, W_r, W_i, b_r, b_i):
    sp = f64(x_crop)
    xr = mxq(sp[:, 0].transpose(1, 2, 0, 3), 3, "e4m3")
    xi = mxq(sp[:, 1].transpose(1, 2, 0, 3), 3, "e4m3")
    wr = mxq(f64(W_r), 2, "e4m3")
    wi = mxq(f64(W_i), 2, "e4m3")
    rr = xr @ wr
    ii = xi @ wi
    ri = xr @ wi
    ir = xi @ wr
    r = rr - ii + f64(b_r)
    i = ri + ir + f64(b_i)
    y = np.stack([r.transpose(2, 0, 1, 3), i.transpose(2, 0, 1, 3)], axis=1)
    return np.maximum(y, 0.0)

@@ -1,0 +1,248 @@
+from contextlib import ExitStack
+
+import concourse.bass as bass
+import concourse.mybir as mybir
+import concourse.tile as tile
+from concourse.masks import make_identity
+
+F32 = mybir.dt.float32
+BF16 = mybir.dt.bfloat16
+U32 = mybir.dt.uint32
+U8 = mybir.dt.uint8
+FP8X4 = mybir.dt.float8_e4m3fn_x4
+ADD = mybir.AluOpType.add
+RELU = mybir.ActivationFunctionType.Relu
+
+P = 128
+B, C, F = 1024, 1024, 256
+NBT = B // P
+NR = 2 * NBT
+FLOPS = 4 * 4 * 2 * B * C * F
+
+MANUAL = True
+LOOK = 2
+XBUFS = 8
+
+
+def tile_dot_pa_t_kernel(tc, x_crop, W_r, W_i, b_r, b_i, out):
+    nc = tc.nc
+    xv = x_crop.rearrange("(t b) r h w c -> t h b r (w c)", b=P)
+    ov = out.rearrange("(t b) r h w f -> t h b r (w f)", b=P)
+    wv = {
+        "r": W_r.rearrange("h w (s p e) f -> h w p s (e f)", s=4, p=P, e=2),
+        "i": W_i.rearrange("h w (s p e) f -> h w p s (e f)", s=4, p=P, e=2),
+    }
+
+    with ExitStack() as ctx:
+        const = ctx.enter_context(tc.tile_pool(name="const", bufs=1))
+        xpool = ctx.enter_context(tc.tile_pool(name="xraw", bufs=XBUFS))
+        wrawp = ctx.enter_context(tc.tile_pool(name="wraw", bufs=8))
+        gwp = ctx.enter_context(tc.tile_pool(name="gw", bufs=2))
+        gxp = ctx.enter_context(tc.tile_pool(name="gx", bufs=3))
+        xcp = ctx.enter_context(tc.tile_pool(name="xc", bufs=4))
+        otp = ctx.enter_context(tc.tile_pool(name="ot", bufs=3))
+        pst = ctx.enter_context(tc.psum_pool(name="pst", bufs=4))
+        psa = ctx.enter_context(tc.psum_pool(name="psa", bufs=4))
+        if MANUAL:
+            ctx.enter_context(tc.manual_schedule())
+
+        wc = const.tile([P, 4 * 1536], U32, align_bytes=64)
+        ws = const.tile([P, 4 * 1536], U8, align_bytes=64)
+        ident = const.tile([P, P], F32)
+        ones = const.tile([P, P], BF16)
+        brow = const.tile([P, 2 * F], BF16)
+        bias = const.tile([P, 2 * F], F32)
+        warm = const.tile([P, 1], F32)
+
+        xraw = {}
+        wraw = {}
+        gws = {}
+        gxs = {}
+        xcs = {}
+        xss = {}
+        accs = {}
+        ots = {}
+
+        def load_w(px, m):
+            t = wrawp.tile([P, 2048], BF16, name="wraw")
+            nc.sync.dma_start(
+                out=t[:].rearrange("p (s k) -> p s k", s=4), in_=wv[m][px // 2, px % 2]
+            )
+            wraw[(px, m)] = t
+
+        def load_x(r):
+            t = xpool.tile([P, 4096], BF16, name="xraw")
+            nc.sync.dma_start(
+                out=t[:].rearrange("p (r k) -> p r k", r=2), in_=xv[r % NBT, r // NBT]
+            )
+            xraw[r] = t
+
+        def regroup_w(px, m, g, eng):
+            if px not in gws:
+                gws[px] = gwp.tile([P, 6144], BF16, name="gw", align_bytes=64)
+            col0 = 256 if m == "r" else 512
+            src = wraw[(px, m)][:, g * 1024 : (g + 1) * 1024].rearrange(
+                "p (t c i) -> p c t i", t=4, i=4
+            )
+            lo = g * 3072 + col0 * 4
+            dst = gws[px][:, lo : lo + 1024].rearrange("p (c i t) -> p c t i", i=4, t=4)
+            if eng == "v":
+                nc.vector.tensor_copy(out=dst, in_=src)
+            else:
+                nc.scalar.copy(out=dst, in_=src)
+
+        def negate_w(px):
+            g3 = gws[px][:].rearrange("p (g m) -> p g m", g=2)
+            nc.vector.tensor_scalar_mul(out=g3[:, :, 0:1024], in0=g3[:, :, 2048:3072], scalar1=-1.0)
+
+        def quant_w(px, part):
+            lo, n = (0, 4096) if part == 0 else (4096, 2048)
+            wlo = px * 1536 + lo // 4
+            nc.vector.quantize_mx(
+                out=wc[:, wlo : wlo + n // 4].bitcast(FP8X4),
+                scales=ws[:, wlo : wlo + n // 4],
+                in_=gws[px][:, lo : lo + n],
+            )
+
+        def transposes(r):
+            xw = xraw[r][:].bitcast(F32)
+            banks = []
+            for un in range(4):
+                w, ri = un // 2, un % 2
+                off = (ri * 2 + w) * 512
+                xt = pst.tile([P, 4, P], F32, name="xt")
+                for j in range(4):
+                    nc.tensor.transpose(xt[:, j, :], xw[:, off + j * P : off + (j + 1) * P], ident[:])
+                banks.append(xt)
+            return banks
+
+        def copies(r, banks, engs):
+            gx = gxp.tile([P, 4096], BF16, name="gx", align_bytes=64)
+            gxs[r] = gx
+            gw32 = gx[:].bitcast(F32)
+            for un in range(4):
+                dst = gw32[:, un * 512 : (un + 1) * 512].rearrange(
+                    "p (g b u) -> p g b u", g=2, b=P, u=2
+                )
+                src = banks[un][:].rearrange("p (g u) b -> p g b u", g=2, u=2)
+                if engs[un] == "v":
+                    nc.vector.tensor_copy(out=dst, in_=src)
+                else:
+                    nc.scalar.copy(out=dst, in_=src)
+
+        def quant_x(r):
+            xc = xcp.tile([P, 1024], U32, name="xc", align_bytes=64)
+            xs = xcp.tile([P, 1024], U8, name="xs", align_bytes=64)
+            xcs[r] = xc
+            xss[r] = xs
+            nc.vector.quantize_mx(out=xc[:].bitcast(FP8X4), scales=xs[:], in_=gxs[r][:])
+
+        def mx(r):
+            h = r // NBT
+            for w in range(2):
+                px = 2 * h + w
+                acc = psa.tile([P, 512], F32, name="acc")
+                accs[(r, w)] = acc
+                k = 0
+                for ri in range(2):
+                    for g in range(2):
+                        lo = (w * 2 + ri) * 256 + g * P
+                        wlo = px * 1536 + g * 768 + (256 if ri == 0 else 0)
+                        nc.tensor.matmul_mx(
+                            out=acc[:],
+                            lhsT=xcs[r][:, lo : lo + P].bitcast(FP8X4),
+                            lhsT_scale=xss[r][:, lo : lo + P],
+                            rhs=wc[:, wlo : wlo + 512].bitcast(FP8X4),
+                            rhs_scale=ws[:, wlo : wlo + 512],
+                            start=(k == 0),
+                            stop=(k == 3),
+                        )
+                        k += 1
+
+        def add_bias(r):
+            ot = otp.tile([P, 2, 2, F], F32, name="ot")
+            ots[r] = ot
+            for w in range(2):
+                nc.vector.tensor_tensor(
+                    out=ot[:, :, w, :],
+                    in0=accs[(r, w)][:].rearrange("p (r f) -> p r f", r=2),
+                    in1=bias[:].rearrange("p (r f) -> p r f", r=2),
+                    op=ADD,
+                )
+
+        def relu_store(r):
+            flat = ots[r][:].rearrange("p r w f -> p (r w f)")
+            nc.scalar.activation(out=flat, in_=flat, func=RELU)
+            nc.sync.dma_start(
+                out=ov[r % NBT, r // NBT], in_=ots[r][:].rearrange("p r w f -> p r (w f)")
+            )
+
+        make_identity(nc, ident[:])
+        nc.vector.memset(ones[:], 1.0)
+        nc.vector.memset(brow[:], 0.0)
+        nc.scalar.dma_start(out=brow[0:1, 0:F], in_=b_r.rearrange("(o f) -> o f", o=1))
+        nc.scalar.dma_start(out=brow[0:1, F : 2 * F], in_=b_i.rearrange("(o f) -> o f", o=1))
+        nc.scalar.activation(out=warm[:], in_=ones[:, 0:1], func=RELU)
+
+        load_w(0, "i")
+        load_w(0, "r")
+        load_x(0)
+        load_w(1, "i")
+        load_w(1, "r")
+        load_x(1)
+        load_x(2)
+        load_w(2, "i")
+        load_x(3)
+        load_w(2, "r")
+        load_x(4)
+        load_w(3, "i")
+        load_x(5)
+        load_w(3, "r")
+        load_x(6)
+        load_x(7)
+
+        for px in range(2):
+            for m in ("i", "r"):
+                for g in range(2):
+                    regroup_w(px, m, g, "v")
+                if m == "i":
+                    negate_w(px)
+            quant_w(px, 0)
+            quant_w(px, 1)
+
+        chunks = []
+        for px in (2, 3):
+            chunks.append([("rg", px, "i", 0), ("rg", px, "i", 1), ("neg", px)])
+            chunks.append([("rg", px, "r", 0), ("rg", px, "r", 1)])
+            chunks.append([("q", px, 0)])
+            chunks.append([("q", px, 1)])
+
+        for s in range(NR + LOOK + 1):
+            if s < NR:
+                banks = transposes(s)
+                if s == 1:
+                    bps = psa.tile([P, 512], F32, name="acc")
+                    nc.tensor.matmul(out=bps[:], lhsT=ones[:], rhs=brow[:], start=True, stop=True)
+                    nc.vector.tensor_copy(out=bias[:], in_=bps[:])
+                if s + XBUFS < NR:
+                    load_x(s + XBUFS)
+            e = s - LOOK - 1
+            if 0 <= e:
+                add_bias(e)
+            if s < NR:
+                busy = 1 <= s <= len(chunks)
+                copies(s, banks, "ssss" if busy or s == 0 else "sssv")
+            if 1 <= s <= NR:
+                quant_x(s - 1)
+            if 1 <= s <= len(chunks):
+                for c in chunks[s - 1]:
+                    if c[0] == "rg":
+                        regroup_w(c[1], c[2], c[3], "v")
+                    elif c[0] == "neg":
+                        negate_w(c[1])
+                    else:
+                        quant_w(c[1], c[2])
+            if 0 <= e:
+                relu_store(e)
+            if 0 <= s - LOOK < NR:
+                mx(s - LOOK)

@@ -1,8 +1,6 @@
 from contextlib import ExitStack
 
-import concourse.bass as bass
 import concourse.mybir as mybir
-import concourse.tile as tile
 from concourse.masks import make_identity
 
 F32 = mybir.dt.float32
@@ -19,15 +17,17 @@ NBT = B // P
 NR = 2 * NBT
 FLOPS = 4 * 4 * 2 * B * C * F
 
-MANUAL = True
 LOOK = 2
 XBUFS = 8
+OBUFS = 8
+W_STEP0 = 4
 
 
 def tile_dot_pa_t_kernel(tc, x_crop, W_r, W_i, b_r, b_i, out):
     nc = tc.nc
     xv = x_crop.rearrange("(t b) r h w c -> t h b r (w c)", b=P)
     ov = out.rearrange("(t b) r h w f -> t h b r (w f)", b=P)
+    ovw = out.rearrange("(t b) r h w f -> t h w b r f", b=P)
     wv = {
         "r": W_r.rearrange("h w (s p e) f -> h w p s (e f)", s=4, p=P, e=2),
         "i": W_i.rearrange("h w (s p e) f -> h w p s (e f)", s=4, p=P, e=2),
@@ -36,15 +36,14 @@ def tile_dot_pa_t_kernel(tc, x_crop, W_r, W_i, b_r, b_i, out):
     with ExitStack() as ctx:
         const = ctx.enter_context(tc.tile_pool(name="const", bufs=1))
         xpool = ctx.enter_context(tc.tile_pool(name="xraw", bufs=XBUFS))
-        wrawp = ctx.enter_context(tc.tile_pool(name="wraw", bufs=8))
+        wrawp = ctx.enter_context(tc.tile_pool(name="wraw", bufs=4))
         gwp = ctx.enter_context(tc.tile_pool(name="gw", bufs=2))
         gxp = ctx.enter_context(tc.tile_pool(name="gx", bufs=3))
         xcp = ctx.enter_context(tc.tile_pool(name="xc", bufs=4))
-        otp = ctx.enter_context(tc.tile_pool(name="ot", bufs=3))
+        otp = ctx.enter_context(tc.tile_pool(name="ot", bufs=OBUFS))
         pst = ctx.enter_context(tc.psum_pool(name="pst", bufs=4))
         psa = ctx.enter_context(tc.psum_pool(name="psa", bufs=4))
-        if MANUAL:
-            ctx.enter_context(tc.manual_schedule())
+        ctx.enter_context(tc.manual_schedule())
 
         wc = const.tile([P, 4 * 1536], U32, align_bytes=64)
         ws = const.tile([P, 4 * 1536], U8, align_bytes=64)
@@ -62,6 +61,7 @@ def tile_dot_pa_t_kernel(tc, x_crop, W_r, W_i, b_r, b_i, out):
         xss = {}
         accs = {}
         ots = {}
+        banks = {}
 
         def load_w(px, m):
             t = wrawp.tile([P, 2048], BF16, name="wraw")
@@ -77,46 +77,43 @@ def tile_dot_pa_t_kernel(tc, x_crop, W_r, W_i, b_r, b_i, out):
             )
             xraw[r] = t
 
-        def regroup_w(px, m, g, eng):
+        def regroup_w(px, m):
             if px not in gws:
                 gws[px] = gwp.tile([P, 6144], BF16, name="gw", align_bytes=64)
             col0 = 256 if m == "r" else 512
-            src = wraw[(px, m)][:, g * 1024 : (g + 1) * 1024].rearrange(
-                "p (t c i) -> p c t i", t=4, i=4
-            )
-            lo = g * 3072 + col0 * 4
-            dst = gws[px][:, lo : lo + 1024].rearrange("p (c i t) -> p c t i", i=4, t=4)
-            if eng == "v":
+            for g in range(2):
+                src = wraw[(px, m)][:, g * 1024 : (g + 1) * 1024].rearrange(
+                    "p (t c i) -> p c t i", t=4, i=4
+                )
+                lo = g * 3072 + col0 * 4
+                dst = gws[px][:, lo : lo + 1024].rearrange("p (c i t) -> p c t i", i=4, t=4)
                 nc.vector.tensor_copy(out=dst, in_=src)
-            else:
-                nc.scalar.copy(out=dst, in_=src)
 
         def negate_w(px):
             g3 = gws[px][:].rearrange("p (g m) -> p g m", g=2)
             nc.vector.tensor_scalar_mul(out=g3[:, :, 0:1024], in0=g3[:, :, 2048:3072], scalar1=-1.0)
 
-        def quant_w(px, part):
-            lo, n = (0, 4096) if part == 0 else (4096, 2048)
-            wlo = px * 1536 + lo // 4
-            nc.vector.quantize_mx(
-                out=wc[:, wlo : wlo + n // 4].bitcast(FP8X4),
-                scales=ws[:, wlo : wlo + n // 4],
-                in_=gws[px][:, lo : lo + n],
-            )
+        def quant_w(px):
+            for lo, n in ((0, 4096), (4096, 2048)):
+                wlo = px * 1536 + lo // 4
+                nc.vector.quantize_mx(
+                    out=wc[:, wlo : wlo + n // 4].bitcast(FP8X4),
+                    scales=ws[:, wlo : wlo + n // 4],
+                    in_=gws[px][:, lo : lo + n],
+                )
 
         def transposes(r):
             xw = xraw[r][:].bitcast(F32)
-            banks = []
+            banks[r] = []
             for un in range(4):
                 w, ri = un // 2, un % 2
                 off = (ri * 2 + w) * 512
                 xt = pst.tile([P, 4, P], F32, name="xt")
                 for j in range(4):
                     nc.tensor.transpose(xt[:, j, :], xw[:, off + j * P : off + (j + 1) * P], ident[:])
-                banks.append(xt)
-            return banks
+                banks[r].append(xt)
 
-        def copies(r, banks, engs):
+        def copies(r, engs):
             gx = gxp.tile([P, 4096], BF16, name="gx", align_bytes=64)
             gxs[r] = gx
             gw32 = gx[:].bitcast(F32)
@@ -124,18 +121,21 @@ def tile_dot_pa_t_kernel(tc, x_crop, W_r, W_i, b_r, b_i, out):
                 dst = gw32[:, un * 512 : (un + 1) * 512].rearrange(
                     "p (g b u) -> p g b u", g=2, b=P, u=2
                 )
-                src = banks[un][:].rearrange("p (g u) b -> p g b u", g=2, u=2)
+                src = banks[r][un][:].rearrange("p (g u) b -> p g b u", g=2, u=2)
                 if engs[un] == "v":
                     nc.vector.tensor_copy(out=dst, in_=src)
                 else:
                     nc.scalar.copy(out=dst, in_=src)
 
-        def quant_x(r):
-            xc = xcp.tile([P, 1024], U32, name="xc", align_bytes=64)
-            xs = xcp.tile([P, 1024], U8, name="xs", align_bytes=64)
-            xcs[r] = xc
-            xss[r] = xs
-            nc.vector.quantize_mx(out=xc[:].bitcast(FP8X4), scales=xs[:], in_=gxs[r][:])
+        def quant_x(r, w):
+            if w == 0:
+                xcs[r] = xcp.tile([P, 1024], U32, name="xc", align_bytes=64)
+                xss[r] = xcp.tile([P, 1024], U8, name="xs", align_bytes=64)
+            nc.vector.quantize_mx(
+                out=xcs[r][:, w * 512 : (w + 1) * 512].bitcast(FP8X4),
+                scales=xss[r][:, w * 512 : (w + 1) * 512],
+                in_=gxs[r][:, w * 2048 : (w + 1) * 2048],
+            )
 
         def mx(r):
             h = r // NBT
@@ -159,16 +159,15 @@ def tile_dot_pa_t_kernel(tc, x_crop, W_r, W_i, b_r, b_i, out):
                         )
                         k += 1
 
-        def add_bias(r):
-            ot = otp.tile([P, 2, 2, F], F32, name="ot")
-            ots[r] = ot
-            for w in range(2):
-                nc.vector.tensor_tensor(
-                    out=ot[:, :, w, :],
-                    in0=accs[(r, w)][:].rearrange("p (r f) -> p r f", r=2),
-                    in1=bias[:].rearrange("p (r f) -> p r f", r=2),
-                    op=ADD,
-                )
+        def add_bias(r, w):
+            if w == 0:
+                ots[r] = otp.tile([P, 2, 2, F], F32, name="ot")
+            nc.vector.tensor_tensor(
+                out=ots[r][:, :, w, :],
+                in0=accs[(r, w)][:].rearrange("p (r f) -> p r f", r=2),
+                in1=bias[:].rearrange("p (r f) -> p r f", r=2),
+                op=ADD,
+            )
 
         def relu_store(r):
             flat = ots[r][:].rearrange("p r w f -> p (r w f)")
@@ -176,6 +175,10 @@ def tile_dot_pa_t_kernel(tc, x_crop, W_r, W_i, b_r, b_i, out):
             nc.sync.dma_start(
                 out=ov[r % NBT, r // NBT], in_=ots[r][:].rearrange("p r w f -> p r (w f)")
             )
+
+        def relu_store_half(r, w):
+            nc.scalar.activation(out=ots[r][:, :, w, :], in_=ots[r][:, :, w, :], func=RELU)
+            nc.sync.dma_start(out=ovw[r % NBT, r // NBT, w], in_=ots[r][:, :, w, :])
 
         make_identity(nc, ident[:])
         nc.vector.memset(ones[:], 1.0)
@@ -189,60 +192,71 @@ def tile_dot_pa_t_kernel(tc, x_crop, W_r, W_i, b_r, b_i, out):
         load_x(0)
         load_w(1, "i")
         load_w(1, "r")
-        load_x(1)
-        load_x(2)
+        for r in range(1, 6):
+            load_x(r)
+
+        regroup_w(0, "i")
+        negate_w(0)
+        regroup_w(0, "r")
+        quant_w(0)
         load_w(2, "i")
-        load_x(3)
         load_w(2, "r")
-        load_x(4)
-        load_w(3, "i")
-        load_x(5)
-        load_w(3, "r")
         load_x(6)
+
+        transposes(0)
+        copies(0, "ssss")
+        quant_x(0, 0)
+        regroup_w(1, "i")
+        negate_w(1)
+        quant_x(0, 1)
+        regroup_w(1, "r")
+        quant_w(1)
+        load_w(3, "i")
+        load_w(3, "r")
         load_x(7)
 
-        for px in range(2):
-            for m in ("i", "r"):
-                for g in range(2):
-                    regroup_w(px, m, g, "v")
-                if m == "i":
-                    negate_w(px)
-            quant_w(px, 0)
-            quant_w(px, 1)
+        transposes(1)
+        bps = psa.tile([P, 512], F32, name="acc")
+        nc.tensor.matmul(out=bps[:], lhsT=ones[:], rhs=brow[:], start=True, stop=True)
+        nc.vector.tensor_copy(out=bias[:], in_=bps[:])
+        copies(1, "ssss")
+        mx(0)
+        transposes(2)
+        for r in range(XBUFS, XBUFS + 3):
+            load_x(r)
+        quant_x(1, 0)
+        quant_x(1, 1)
+        copies(2, "ssss")
 
-        chunks = []
-        for px in (2, 3):
-            chunks.append([("rg", px, "i", 0), ("rg", px, "i", 1), ("neg", px)])
-            chunks.append([("rg", px, "r", 0), ("rg", px, "r", 1)])
-            chunks.append([("q", px, 0)])
-            chunks.append([("q", px, 1)])
-
-        for s in range(NR + LOOK + 1):
+        for s in range(3, NR + LOOK + 1):
+            e = s - LOOK - 1
+            wstep = s - W_STEP0
             if s < NR:
-                banks = transposes(s)
-                if s == 1:
-                    bps = psa.tile([P, 512], F32, name="acc")
-                    nc.tensor.matmul(out=bps[:], lhsT=ones[:], rhs=brow[:], start=True, stop=True)
-                    nc.vector.tensor_copy(out=bias[:], in_=bps[:])
+                transposes(s)
                 if s + XBUFS < NR:
                     load_x(s + XBUFS)
-            e = s - LOOK - 1
-            if 0 <= e:
-                add_bias(e)
+            if e < NR - 1:
+                add_bias(e, 0)
+                add_bias(e, 1)
             if s < NR:
-                busy = 1 <= s <= len(chunks)
-                copies(s, banks, "ssss" if busy or s == 0 else "sssv")
-            if 1 <= s <= NR:
-                quant_x(s - 1)
-            if 1 <= s <= len(chunks):
-                for c in chunks[s - 1]:
-                    if c[0] == "rg":
-                        regroup_w(c[1], c[2], c[3], "v")
-                    elif c[0] == "neg":
-                        negate_w(c[1])
-                    else:
-                        quant_w(c[1], c[2])
-            if 0 <= e:
+                copies(s, "ssss" if wstep < 6 else "sssv")
+            if s - 1 < NR:
+                quant_x(s - 1, 0)
+                quant_x(s - 1, 1)
+            if 0 <= wstep < 6:
+                px = 2 + wstep // 3
+                if wstep % 3 == 0:
+                    regroup_w(px, "i")
+                    negate_w(px)
+                elif wstep % 3 == 1:
+                    regroup_w(px, "r")
+                else:
+                    quant_w(px)
+            if e < NR - 1:
                 relu_store(e)
-            if 0 <= s - LOOK < NR:
+            else:
+                for w in range(2):
+                    add_bias(e, w)
+                    relu_store_half(e, w)
+            if s - LOOK < NR:
                 mx(s - LOOK)

@@ -77,7 +77,7 @@ def tile_dot_pa_t_kernel(tc, x_crop, W_r, W_i, b_r, b_i, out):
             )
             xraw[r] = t
 
-        def regroup_w(px, m):
+        def regroup_w(px, m, eng="v"):
             if px not in gws:
                 gws[px] = gwp.tile([P, 6144], BF16, name="gw", align_bytes=64)
             col0 = 256 if m == "r" else 512
@@ -87,7 +87,10 @@ def tile_dot_pa_t_kernel(tc, x_crop, W_r, W_i, b_r, b_i, out):
                 )
                 lo = g * 3072 + col0 * 4
                 dst = gws[px][:, lo : lo + 1024].rearrange("p (c i t) -> p c t i", i=4, t=4)
-                nc.vector.tensor_copy(out=dst, in_=src)
+                if eng == "v":
+                    nc.vector.tensor_copy(out=dst, in_=src)
+                else:
+                    nc.scalar.copy(out=dst, in_=src)
 
         def negate_w(px):
             g3 = gws[px][:].rearrange("p (g m) -> p g m", g=2)
@@ -137,27 +140,32 @@ def tile_dot_pa_t_kernel(tc, x_crop, W_r, W_i, b_r, b_i, out):
                 in_=gxs[r][:, w * 2048 : (w + 1) * 2048],
             )
 
+        def mx_group(r, w, acc, c0, n):
+            px = 2 * (r // NBT) + w
+            k = 0
+            for ri in range(2):
+                for g in range(2):
+                    lo = (w * 2 + ri) * 256 + g * P
+                    wlo = px * 1536 + g * 768 + (256 if ri == 0 else 0) + c0
+                    nc.tensor.matmul_mx(
+                        out=acc,
+                        lhsT=xcs[r][:, lo : lo + P].bitcast(FP8X4),
+                        lhsT_scale=xss[r][:, lo : lo + P],
+                        rhs=wc[:, wlo : wlo + n].bitcast(FP8X4),
+                        rhs_scale=ws[:, wlo : wlo + n],
+                        start=(k == 0),
+                        stop=(k == 3),
+                    )
+                    k += 1
+
+        def mx_bank(r, w):
+            acc = psa.tile([P, 512], F32, name="acc")
+            accs[(r, w)] = acc
+            mx_group(r, w, acc[:], 0, 512)
+
         def mx(r):
-            h = r // NBT
-            for w in range(2):
-                px = 2 * h + w
-                acc = psa.tile([P, 512], F32, name="acc")
-                accs[(r, w)] = acc
-                k = 0
-                for ri in range(2):
-                    for g in range(2):
-                        lo = (w * 2 + ri) * 256 + g * P
-                        wlo = px * 1536 + g * 768 + (256 if ri == 0 else 0)
-                        nc.tensor.matmul_mx(
-                            out=acc[:],
-                            lhsT=xcs[r][:, lo : lo + P].bitcast(FP8X4),
-                            lhsT_scale=xss[r][:, lo : lo + P],
-                            rhs=wc[:, wlo : wlo + 512].bitcast(FP8X4),
-                            rhs_scale=ws[:, wlo : wlo + 512],
-                            start=(k == 0),
-                            stop=(k == 3),
-                        )
-                        k += 1
+            mx_bank(r, 0)
+            mx_bank(r, 1)
 
         def add_bias(r, w):
             if w == 0:
@@ -179,6 +187,14 @@ def tile_dot_pa_t_kernel(tc, x_crop, W_r, W_i, b_r, b_i, out):
         def relu_store_half(r, w):
             nc.scalar.activation(out=ots[r][:, :, w, :], in_=ots[r][:, :, w, :], func=RELU)
             nc.sync.dma_start(out=ovw[r % NBT, r // NBT, w], in_=ots[r][:, :, w, :])
+
+        def last_piece(r, ri):
+            piece = ots[r][:, ri, 1, :]
+            nc.vector.tensor_tensor(
+                out=piece, in0=accs[(r, 1, ri)][:], in1=bias[:, ri * F : (ri + 1) * F], op=ADD
+            )
+            nc.scalar.activation(out=piece, in_=piece, func=RELU)
+            nc.sync.dma_start(out=ovw[r % NBT, r // NBT, 1][:, ri, :], in_=piece)
 
         make_identity(nc, ident[:])
         nc.vector.memset(ones[:], 1.0)
@@ -205,22 +221,23 @@ def tile_dot_pa_t_kernel(tc, x_crop, W_r, W_i, b_r, b_i, out):
 
         transposes(0)
         copies(0, "ssss")
-        quant_x(0, 0)
         regroup_w(1, "i")
+        quant_x(0, 0)
         negate_w(1)
         quant_x(0, 1)
-        regroup_w(1, "r")
+        regroup_w(1, "r", "s")
         quant_w(1)
         load_w(3, "i")
         load_w(3, "r")
         load_x(7)
 
+        mx_bank(0, 0)
         transposes(1)
         bps = psa.tile([P, 512], F32, name="acc")
         nc.tensor.matmul(out=bps[:], lhsT=ones[:], rhs=brow[:], start=True, stop=True)
         nc.vector.tensor_copy(out=bias[:], in_=bps[:])
         copies(1, "ssss")
-        mx(0)
+        mx_bank(0, 1)
         transposes(2)
         for r in range(XBUFS, XBUFS + 3):
             load_x(r)
@@ -255,8 +272,14 @@ def tile_dot_pa_t_kernel(tc, x_crop, W_r, W_i, b_r, b_i, out):
             if e < NR - 1:
                 relu_store(e)
             else:
-                for w in range(2):
-                    add_bias(e, w)
-                    relu_store_half(e, w)
-            if s - LOOK < NR:
+                add_bias(e, 0)
+                relu_store_half(e, 0)
+                for ri in range(2):
+                    last_piece(e, ri)
+            if s - LOOK < NR - 1:
                 mx(s - LOOK)
+            elif s - LOOK == NR - 1:
+                mx_bank(NR - 1, 0)
+                for ri in range(2):
+                    accs[(NR - 1, 1, ri)] = psa.tile([P, F], F32, name="acc")
+                    mx_group(NR - 1, 1, accs[(NR - 1, 1, ri)][:], ri * F, F)

@@ -196,6 +196,16 @@ def tile_dot_pa_t_kernel(tc, x_crop, W_r, W_i, b_r, b_i, out):
             nc.scalar.activation(out=piece, in_=piece, func=RELU)
             nc.sync.dma_start(out=ovw[r % NBT, r // NBT, 1][:, ri, :], in_=piece)
 
+        def keep_clock(px, m, n):
+            for j in range(n):
+                nc.tensor.matmul(
+                    out=spare[:],
+                    lhsT=ones[:],
+                    rhs=wraw[(px, m)][:, (j % 4) * 512 : (j % 4 + 1) * 512],
+                    start=True,
+                    stop=True,
+                )
+
         make_identity(nc, ident[:])
         nc.vector.memset(ones[:], 1.0)
         nc.vector.memset(brow[:], 0.0)
@@ -211,6 +221,9 @@ def tile_dot_pa_t_kernel(tc, x_crop, W_r, W_i, b_r, b_i, out):
         for r in range(1, 6):
             load_x(r)
 
+        spare = psa.tile([P, 512], F32, name="acc")
+        keep_clock(0, "i", 3)
+        keep_clock(0, "r", 4)
         regroup_w(0, "i")
         negate_w(0)
         regroup_w(0, "r")
@@ -220,6 +233,7 @@ def tile_dot_pa_t_kernel(tc, x_crop, W_r, W_i, b_r, b_i, out):
         load_x(6)
 
         transposes(0)
+        keep_clock(1, "i", 3)
         copies(0, "ssss")
         regroup_w(1, "i")
         quant_x(0, 0)

@@ -105,10 +105,11 @@ def tile_dot_pa_t_kernel(tc, x_crop, W_r, W_i, b_r, b_i, out):
                     in_=gws[px][:, lo : lo + n],
                 )
 
-        def transposes(r):
+        def transposes(r, uns=(0, 1, 2, 3)):
             xw = xraw[r][:].bitcast(F32)
-            banks[r] = []
-            for un in range(4):
+            if uns[0] == 0:
+                banks[r] = []
+            for un in uns:
                 w, ri = un // 2, un % 2
                 off = (ri * 2 + w) * 512
                 xt = pst.tile([P, 4, P], F32, name="xt")
@@ -262,13 +263,16 @@ def tile_dot_pa_t_kernel(tc, x_crop, W_r, W_i, b_r, b_i, out):
         for s in range(3, NR + LOOK + 1):
             e = s - LOOK - 1
             wstep = s - W_STEP0
-            if s < NR:
-                transposes(s)
-                if s + XBUFS < NR:
-                    load_x(s + XBUFS)
             if e < NR - 1:
                 add_bias(e, 0)
                 add_bias(e, 1)
+            if s < NR:
+                transposes(s, (0, 1))
+                mx_bank(s - LOOK, 0)
+                transposes(s, (2, 3))
+                mx_bank(s - LOOK, 1)
+                if s + XBUFS < NR:
+                    load_x(s + XBUFS)
             if s < NR:
                 copies(s, "ssss" if wstep < 6 else "sssv")
             if s - 1 < NR:
@@ -290,7 +294,9 @@ def tile_dot_pa_t_kernel(tc, x_crop, W_r, W_i, b_r, b_i, out):
                 relu_store_half(e, 0)
                 for ri in range(2):
                     last_piece(e, ri)
-            if s - LOOK < NR - 1:
+            if s < NR:
+                pass
+            elif s - LOOK < NR - 1:
                 mx(s - LOOK)
             elif s - LOOK == NR - 1:
                 mx_bank(NR - 1, 0)

@@ -14,32 +14,43 @@ RELU = mybir.ActivationFunctionType.Relu
 P = 128
 B, C, F = 1024, 1024, 256
 NBT = B // P
-NR = 2 * NBT
 FLOPS = 4 * 4 * 2 * B * C * F
 
-LOOK = 2
 XBUFS = 8
-OBUFS = 8
-W_STEP0 = 4
+OBUFS = 12
+GROUPS = [1] * 32
+W1_FIRST = 4
+W2_FIRST = 10
+W_DONE = 21
+LAG = 2
+W_LOAD_AFTER = 4
 
 
 def tile_dot_pa_t_kernel(tc, x_crop, W_r, W_i, b_r, b_i, out):
     nc = tc.nc
     xv = x_crop.rearrange("(t b) r h w c -> t h b r (w c)", b=P)
+    xvw = x_crop.rearrange("(t b) r h w c -> t h w b r c", b=P)
     ov = out.rearrange("(t b) r h w f -> t h b r (w f)", b=P)
     ovw = out.rearrange("(t b) r h w f -> t h w b r f", b=P)
     wv = {
         "r": W_r.rearrange("h w (s p e) f -> h w p s (e f)", s=4, p=P, e=2),
         "i": W_i.rearrange("h w (s p e) f -> h w p s (e f)", s=4, p=P, e=2),
     }
+    units = [(0, w, t) for w in range(2) for t in range(NBT)]
+    for i in range(NBT + LAG):
+        if i < NBT:
+            units.append((1, 0, i))
+        if i >= LAG:
+            units.append((1, 1, i - LAG))
+    NU = len(units)
 
     with ExitStack() as ctx:
         const = ctx.enter_context(tc.tile_pool(name="const", bufs=1))
         xpool = ctx.enter_context(tc.tile_pool(name="xraw", bufs=XBUFS))
         wrawp = ctx.enter_context(tc.tile_pool(name="wraw", bufs=4))
         gwp = ctx.enter_context(tc.tile_pool(name="gw", bufs=2))
-        gxp = ctx.enter_context(tc.tile_pool(name="gx", bufs=3))
-        xcp = ctx.enter_context(tc.tile_pool(name="xc", bufs=4))
+        gxp = ctx.enter_context(tc.tile_pool(name="gx", bufs=4))
+        xcp = ctx.enter_context(tc.tile_pool(name="xc", bufs=6))
         otp = ctx.enter_context(tc.tile_pool(name="ot", bufs=OBUFS))
         pst = ctx.enter_context(tc.psum_pool(name="pst", bufs=4))
         psa = ctx.enter_context(tc.psum_pool(name="psa", bufs=4))
@@ -62,96 +73,124 @@ def tile_dot_pa_t_kernel(tc, x_crop, W_r, W_i, b_r, b_i, out):
         accs = {}
         ots = {}
         banks = {}
+        w_ready = [0]
 
-        def load_w(px, m):
-            t = wrawp.tile([P, 2048], BF16, name="wraw")
+        def load_w(px):
+            for m in ("i", "r"):
+                t = wrawp.tile([P, 2048], BF16, name="wraw")
+                nc.sync.dma_start(
+                    out=t[:].rearrange("p (s k) -> p s k", s=4), in_=wv[m][px // 2, px % 2]
+                )
+                wraw[(px, m)] = t
+
+        def load_x_half(h, w, t):
+            if (h, t) not in xraw:
+                xraw[(h, t)] = xpool.tile([P, 4096], BF16, name="xraw")
             nc.sync.dma_start(
-                out=t[:].rearrange("p (s k) -> p s k", s=4), in_=wv[m][px // 2, px % 2]
+                out=xraw[(h, t)][:].rearrange("p (r w c) -> p r w c", r=2, w=2)[:, :, w, :],
+                in_=xvw[t, h, w],
             )
-            wraw[(px, m)] = t
 
-        def load_x(r):
-            t = xpool.tile([P, 4096], BF16, name="xraw")
+        def load_x(h, t):
+            xraw[(h, t)] = xpool.tile([P, 4096], BF16, name="xraw")
             nc.sync.dma_start(
-                out=t[:].rearrange("p (r k) -> p r k", r=2), in_=xv[r % NBT, r // NBT]
+                out=xraw[(h, t)][:].rearrange("p (r k) -> p r k", r=2), in_=xv[t, h]
             )
-            xraw[r] = t
 
-        def regroup_w(px, m, eng="v"):
+        def regroup_w(px, m, g, eng="v"):
             if px not in gws:
                 gws[px] = gwp.tile([P, 6144], BF16, name="gw", align_bytes=64)
             col0 = 256 if m == "r" else 512
-            for g in range(2):
-                src = wraw[(px, m)][:, g * 1024 : (g + 1) * 1024].rearrange(
-                    "p (t c i) -> p c t i", t=4, i=4
-                )
-                lo = g * 3072 + col0 * 4
-                dst = gws[px][:, lo : lo + 1024].rearrange("p (c i t) -> p c t i", i=4, t=4)
-                if eng == "v":
-                    nc.vector.tensor_copy(out=dst, in_=src)
-                else:
-                    nc.scalar.copy(out=dst, in_=src)
+            src = wraw[(px, m)][:, g * 1024 : (g + 1) * 1024].rearrange(
+                "p (t c i) -> p c t i", t=4, i=4
+            )
+            lo = g * 3072 + col0 * 4
+            dst = gws[px][:, lo : lo + 1024].rearrange("p (c i t) -> p c t i", i=4, t=4)
+            if eng == "v":
+                nc.vector.tensor_copy(out=dst, in_=src)
+            else:
+                nc.scalar.copy(out=dst, in_=src)
 
         def negate_w(px):
             g3 = gws[px][:].rearrange("p (g m) -> p g m", g=2)
             nc.vector.tensor_scalar_mul(out=g3[:, :, 0:1024], in0=g3[:, :, 2048:3072], scalar1=-1.0)
 
-        def quant_w(px):
-            for lo, n in ((0, 4096), (4096, 2048)):
-                wlo = px * 1536 + lo // 4
-                nc.vector.quantize_mx(
-                    out=wc[:, wlo : wlo + n // 4].bitcast(FP8X4),
-                    scales=ws[:, wlo : wlo + n // 4],
-                    in_=gws[px][:, lo : lo + n],
-                )
+        def quant_w(px, j):
+            wlo = px * 1536 + j * 512
+            nc.vector.quantize_mx(
+                out=wc[:, wlo : wlo + 512].bitcast(FP8X4),
+                scales=ws[:, wlo : wlo + 512],
+                in_=gws[px][:, j * 2048 : (j + 1) * 2048],
+            )
 
-        def transposes(r, uns=(0, 1, 2, 3)):
-            xw = xraw[r][:].bitcast(F32)
-            if uns[0] == 0:
-                banks[r] = []
-            for un in uns:
-                w, ri = un // 2, un % 2
+        def w_part(px, k):
+            if k == 0:
+                regroup_w(px, "i", 0)
+            elif k == 1:
+                regroup_w(px, "i", 1)
+            elif k == 2:
+                regroup_w(px, "r", 0)
+                regroup_w(px, "r", 1, "s")
+                if px == 1:
+                    load_w(3)
+            elif k == 3:
+                negate_w(px)
+            else:
+                quant_w(px, k - 4)
+                if k == 6:
+                    w_ready.append(px)
+
+        w_plan = {}
+        for k in range(7):
+            w_plan.setdefault(W1_FIRST + (6 * k) // 7, []).append((1, k))
+        for k in range(14):
+            w_plan.setdefault(W2_FIRST + (11 * k) // 14, []).append((2 + k // 7, k % 7))
+
+        def w_work(c):
+            for px, k in w_plan.get(c, []):
+                w_part(px, k)
+
+        def transposes(u):
+            h, w, t = units[u]
+            xw = xraw[(h, t)][:].bitcast(F32)
+            banks[u] = []
+            for ri in range(2):
                 off = (ri * 2 + w) * 512
                 xt = pst.tile([P, 4, P], F32, name="xt")
                 for j in range(4):
                     nc.tensor.transpose(xt[:, j, :], xw[:, off + j * P : off + (j + 1) * P], ident[:])
-                banks[r].append(xt)
+                banks[u].append(xt)
 
-        def copies(r, engs):
-            gx = gxp.tile([P, 4096], BF16, name="gx", align_bytes=64)
-            gxs[r] = gx
-            gw32 = gx[:].bitcast(F32)
-            for un in range(4):
-                dst = gw32[:, un * 512 : (un + 1) * 512].rearrange(
-                    "p (g b u) -> p g b u", g=2, b=P, u=2
-                )
-                src = banks[r][un][:].rearrange("p (g u) b -> p g b u", g=2, u=2)
-                if engs[un] == "v":
-                    nc.vector.tensor_copy(out=dst, in_=src)
-                else:
-                    nc.scalar.copy(out=dst, in_=src)
-
-        def quant_x(r, w):
-            if w == 0:
-                xcs[r] = xcp.tile([P, 1024], U32, name="xc", align_bytes=64)
-                xss[r] = xcp.tile([P, 1024], U8, name="xs", align_bytes=64)
-            nc.vector.quantize_mx(
-                out=xcs[r][:, w * 512 : (w + 1) * 512].bitcast(FP8X4),
-                scales=xss[r][:, w * 512 : (w + 1) * 512],
-                in_=gxs[r][:, w * 2048 : (w + 1) * 2048],
+        def copy_x(u, ri, eng):
+            if ri == 0:
+                gxs[u] = gxp.tile([P, 2048], BF16, name="gx", align_bytes=64)
+            dst = gxs[u][:].bitcast(F32)[:, ri * 512 : (ri + 1) * 512].rearrange(
+                "p (g b u) -> p g b u", g=2, b=P, u=2
             )
+            src = banks[u][ri][:].rearrange("p (g u) b -> p g b u", g=2, u=2)
+            if eng == "v":
+                nc.vector.tensor_copy(out=dst, in_=src)
+            else:
+                nc.scalar.copy(out=dst, in_=src)
 
-        def mx_group(r, w, acc, c0, n):
-            px = 2 * (r // NBT) + w
+        def quant_x(u):
+            xcs[u] = xcp.tile([P, 512], U32, name="xc", align_bytes=64)
+            xss[u] = xcp.tile([P, 512], U8, name="xs", align_bytes=64)
+            nc.vector.quantize_mx(out=xcs[u][:].bitcast(FP8X4), scales=xss[u][:], in_=gxs[u][:])
+
+        def mx_group(u, acc, c0, n):
+            h, w, t = units[u]
+            px = 2 * h + w
+            assert px in w_ready
             k = 0
             for ri in range(2):
                 for g in range(2):
-                    lo = (w * 2 + ri) * 256 + g * P
+                    lo = ri * 256 + g * P
                     wlo = px * 1536 + g * 768 + (256 if ri == 0 else 0) + c0
                     nc.tensor.matmul_mx(
                         out=acc,
-                        lhsT=xcs[r][:, lo : lo + P].bitcast(FP8X4),
-                        lhsT_scale=xss[r][:, lo : lo + P],
+                        lhsT=xcs[u][:, lo : lo + P].bitcast(FP8X4),
+                        lhsT_scale=xss[u][:, lo : lo + P],
                         rhs=wc[:, wlo : wlo + n].bitcast(FP8X4),
                         rhs_scale=ws[:, wlo : wlo + n],
                         start=(k == 0),
@@ -159,43 +198,46 @@ def tile_dot_pa_t_kernel(tc, x_crop, W_r, W_i, b_r, b_i, out):
                     )
                     k += 1
 
-        def mx_bank(r, w):
-            acc = psa.tile([P, 512], F32, name="acc")
-            accs[(r, w)] = acc
-            mx_group(r, w, acc[:], 0, 512)
+        def mx_unit(u):
+            if u == NU - 1:
+                for ri in range(2):
+                    accs[(u, ri)] = psa.tile([P, F], F32, name="acc")
+                    mx_group(u, accs[(u, ri)][:], ri * F, F)
+            else:
+                accs[u] = psa.tile([P, 512], F32, name="acc")
+                mx_group(u, accs[u][:], 0, 512)
 
-        def mx(r):
-            mx_bank(r, 0)
-            mx_bank(r, 1)
-
-        def add_bias(r, w):
+        def add_bias(u):
+            h, w, t = units[u]
             if w == 0:
-                ots[r] = otp.tile([P, 2, 2, F], F32, name="ot")
+                ots[(h, t)] = otp.tile([P, 2, 2, F], F32, name="ot")
+            o = ots[(h, t)]
+            if u == NU - 1:
+                return
             nc.vector.tensor_tensor(
-                out=ots[r][:, :, w, :],
-                in0=accs[(r, w)][:].rearrange("p (r f) -> p r f", r=2),
+                out=o[:, :, w, :],
+                in0=accs[u][:].rearrange("p (r f) -> p r f", r=2),
                 in1=bias[:].rearrange("p (r f) -> p r f", r=2),
                 op=ADD,
             )
 
-        def relu_store(r):
-            flat = ots[r][:].rearrange("p r w f -> p (r w f)")
-            nc.scalar.activation(out=flat, in_=flat, func=RELU)
-            nc.sync.dma_start(
-                out=ov[r % NBT, r // NBT], in_=ots[r][:].rearrange("p r w f -> p r (w f)")
-            )
-
-        def relu_store_half(r, w):
-            nc.scalar.activation(out=ots[r][:, :, w, :], in_=ots[r][:, :, w, :], func=RELU)
-            nc.sync.dma_start(out=ovw[r % NBT, r // NBT, w], in_=ots[r][:, :, w, :])
-
-        def last_piece(r, ri):
-            piece = ots[r][:, ri, 1, :]
-            nc.vector.tensor_tensor(
-                out=piece, in0=accs[(r, 1, ri)][:], in1=bias[:, ri * F : (ri + 1) * F], op=ADD
-            )
-            nc.scalar.activation(out=piece, in_=piece, func=RELU)
-            nc.sync.dma_start(out=ovw[r % NBT, r // NBT, 1][:, ri, :], in_=piece)
+        def relu_store(u):
+            h, w, t = units[u]
+            o = ots[(h, t)]
+            if u == NU - 1:
+                for ri in range(2):
+                    piece = o[:, ri, 1, :]
+                    nc.vector.tensor_tensor(
+                        out=piece, in0=accs[(u, ri)][:], in1=bias[:, ri * F : (ri + 1) * F], op=ADD
+                    )
+                    nc.scalar.activation(out=piece, in_=piece, func=RELU)
+                    nc.sync.dma_start(out=ovw[t, h, 1][:, ri, :], in_=piece)
+                return
+            nc.scalar.activation(out=o[:, :, w, :], in_=o[:, :, w, :], func=RELU)
+            if h == 1 and t >= NBT - 1 - LAG:
+                nc.sync.dma_start(out=ovw[t, h, w], in_=o[:, :, w, :])
+            elif w == 1:
+                nc.sync.dma_start(out=ov[t, h], in_=o[:].rearrange("p r w f -> p r (w f)"))
 
         def keep_clock(px, m, n):
             for j in range(n):
@@ -214,92 +256,55 @@ def tile_dot_pa_t_kernel(tc, x_crop, W_r, W_i, b_r, b_i, out):
         nc.scalar.dma_start(out=brow[0:1, F : 2 * F], in_=b_i.rearrange("(o f) -> o f", o=1))
         nc.scalar.activation(out=warm[:], in_=ones[:, 0:1], func=RELU)
 
-        load_w(0, "i")
-        load_w(0, "r")
-        load_x(0)
-        load_w(1, "i")
-        load_w(1, "r")
-        for r in range(1, 6):
-            load_x(r)
+        load_w(0)
+        for t in range(NBT):
+            if t == W_LOAD_AFTER:
+                load_w(1)
+            load_x_half(0, 0, t)
+        for t in range(NBT // 2):
+            load_x_half(0, 1, t)
 
         spare = psa.tile([P, 512], F32, name="acc")
         keep_clock(0, "i", 3)
         keep_clock(0, "r", 4)
-        regroup_w(0, "i")
-        negate_w(0)
-        regroup_w(0, "r")
-        quant_w(0)
-        load_w(2, "i")
-        load_w(2, "r")
-        load_x(6)
-
-        transposes(0)
-        keep_clock(1, "i", 3)
-        copies(0, "ssss")
-        regroup_w(1, "i")
-        quant_x(0, 0)
-        negate_w(1)
-        quant_x(0, 1)
-        regroup_w(1, "r", "s")
-        quant_w(1)
-        load_w(3, "i")
-        load_w(3, "r")
-        load_x(7)
-
-        mx_bank(0, 0)
-        transposes(1)
         bps = psa.tile([P, 512], F32, name="acc")
         nc.tensor.matmul(out=bps[:], lhsT=ones[:], rhs=brow[:], start=True, stop=True)
+        regroup_w(0, "i", 0)
+        regroup_w(0, "i", 1)
+        regroup_w(0, "r", 0)
+        regroup_w(0, "r", 1, "s")
+        negate_w(0)
+        for j in range(3):
+            quant_w(0, j)
         nc.vector.tensor_copy(out=bias[:], in_=bps[:])
-        copies(1, "ssss")
-        mx_bank(0, 1)
-        transposes(2)
-        for r in range(XBUFS, XBUFS + 3):
-            load_x(r)
-        quant_x(1, 0)
-        quant_x(1, 1)
-        copies(2, "ssss")
+        load_w(2)
+        for t in range(NBT // 2, NBT):
+            load_x_half(0, 1, t)
 
-        for s in range(3, NR + LOOK + 1):
-            e = s - LOOK - 1
-            wstep = s - W_STEP0
-            if e < NR - 1:
-                add_bias(e, 0)
-                add_bias(e, 1)
-            if s < NR:
-                transposes(s, (0, 1))
-                mx_bank(s - LOOK, 0)
-                transposes(s, (2, 3))
-                mx_bank(s - LOOK, 1)
-                if s + XBUFS < NR:
-                    load_x(s + XBUFS)
-            if s < NR:
-                copies(s, "ssss" if wstep < 6 else "sssv")
-            if s - 1 < NR:
-                quant_x(s - 1, 0)
-                quant_x(s - 1, 1)
-            if 0 <= wstep < 6:
-                px = 2 + wstep // 3
-                if wstep % 3 == 0:
-                    regroup_w(px, "i")
-                    negate_w(px)
-                elif wstep % 3 == 1:
-                    regroup_w(px, "r")
-                else:
-                    quant_w(px)
-            if e < NR - 1:
-                relu_store(e)
-            else:
-                add_bias(e, 0)
-                relu_store_half(e, 0)
-                for ri in range(2):
-                    last_piece(e, ri)
-            if s < NR:
-                pass
-            elif s - LOOK < NR - 1:
-                mx(s - LOOK)
-            elif s - LOOK == NR - 1:
-                mx_bank(NR - 1, 0)
-                for ri in range(2):
-                    accs[(NR - 1, 1, ri)] = psa.tile([P, F], F32, name="acc")
-                    mx_group(NR - 1, 1, accs[(NR - 1, 1, ri)][:], ri * F, F)
+        starts = [sum(GROUPS[:j]) for j in range(len(GROUPS) + 1)]
+        NG = len(GROUPS)
+
+        def group(j):
+            return list(range(starts[j], starts[j + 1])) if 0 <= j < NG else []
+
+        for c in range(NG + 4):
+            for u in group(c):
+                transposes(u)
+                h, w, t = units[u]
+                if (h, w) == (0, 1):
+                    load_x(1, t)
+            for u in group(c):
+                copy_x(u, 0, "s")
+                copy_x(u, 1, "s" if c < W_DONE else "v")
+            for u in group(c - 1):
+                quant_x(u)
+            w_work(c)
+            for u in group(c - 3):
+                add_bias(u)
+            for u in group(c - 4):
+                if u < NU - 1:
+                    relu_store(u)
+            if c - 3 == NU - 1:
+                relu_store(NU - 1)
+            for u in group(c - 2):
+                mx_unit(u)

@@ -65,6 +65,7 @@ def tile_dot_pa_t_kernel(tc, x_crop, W_r, W_i, b_r, b_i, out):
         warm = const.tile([P, 1], F32)
 
         xraw = {}
+        xhalf = {}
         wraw = {}
         gws = {}
         gxs = {}
@@ -73,7 +74,7 @@ def tile_dot_pa_t_kernel(tc, x_crop, W_r, W_i, b_r, b_i, out):
         accs = {}
         ots = {}
         banks = {}
-        w_ready = [0]
+        w_ready = []
 
         def load_w(px):
             for m in ("i", "r"):
@@ -83,12 +84,10 @@ def tile_dot_pa_t_kernel(tc, x_crop, W_r, W_i, b_r, b_i, out):
                 )
                 wraw[(px, m)] = t
 
-        def load_x_half(h, w, t):
-            if (h, t) not in xraw:
-                xraw[(h, t)] = xpool.tile([P, 4096], BF16, name="xraw")
+        def load_x_half(w, t):
+            xhalf[(w, t)] = xpool.tile([P, 4096], BF16, name="xraw")
             nc.sync.dma_start(
-                out=xraw[(h, t)][:].rearrange("p (r w c) -> p r w c", r=2, w=2)[:, :, w, :],
-                in_=xvw[t, h, w],
+                out=xhalf[(w, t)][:, 0:2048].rearrange("p (r c) -> p r c", r=2), in_=xvw[t, 0, w]
             )
 
         def load_x(h, t):
@@ -129,14 +128,14 @@ def tile_dot_pa_t_kernel(tc, x_crop, W_r, W_i, b_r, b_i, out):
             elif k == 1:
                 regroup_w(px, "i", 1)
             elif k == 2:
+                negate_w(px)
+            elif k == 3:
                 regroup_w(px, "r", 0)
                 regroup_w(px, "r", 1, "s")
                 if px == 1:
                     load_w(3)
-            elif k == 3:
-                negate_w(px)
             else:
-                quant_w(px, k - 4)
+                quant_w(px, (1, 0, 2)[k - 4])
                 if k == 6:
                     w_ready.append(px)
 
@@ -152,10 +151,10 @@ def tile_dot_pa_t_kernel(tc, x_crop, W_r, W_i, b_r, b_i, out):
 
         def transposes(u):
             h, w, t = units[u]
-            xw = xraw[(h, t)][:].bitcast(F32)
+            xw = (xhalf[(w, t)][:, 0:2048] if h == 0 else xraw[(h, t)][:]).bitcast(F32)
             banks[u] = []
             for ri in range(2):
-                off = (ri * 2 + w) * 512
+                off = ri * 512 if h == 0 else (ri * 2 + w) * 512
                 xt = pst.tile([P, 4, P], F32, name="xt")
                 for j in range(4):
                     nc.tensor.transpose(xt[:, j, :], xw[:, off + j * P : off + (j + 1) * P], ident[:])
@@ -260,26 +259,16 @@ def tile_dot_pa_t_kernel(tc, x_crop, W_r, W_i, b_r, b_i, out):
         for t in range(NBT):
             if t == W_LOAD_AFTER:
                 load_w(1)
-            load_x_half(0, 0, t)
-        for t in range(NBT // 2):
-            load_x_half(0, 1, t)
+            load_x_half(0, t)
 
         spare = psa.tile([P, 512], F32, name="acc")
         keep_clock(0, "i", 3)
         keep_clock(0, "r", 4)
         bps = psa.tile([P, 512], F32, name="acc")
         nc.tensor.matmul(out=bps[:], lhsT=ones[:], rhs=brow[:], start=True, stop=True)
-        regroup_w(0, "i", 0)
-        regroup_w(0, "i", 1)
-        regroup_w(0, "r", 0)
-        regroup_w(0, "r", 1, "s")
-        negate_w(0)
-        for j in range(3):
-            quant_w(0, j)
+        for k in range(7):
+            w_part(0, k)
         nc.vector.tensor_copy(out=bias[:], in_=bps[:])
-        load_w(2)
-        for t in range(NBT // 2, NBT):
-            load_x_half(0, 1, t)
 
         starts = [sum(GROUPS[:j]) for j in range(len(GROUPS) + 1)]
         NG = len(GROUPS)
@@ -291,7 +280,11 @@ def tile_dot_pa_t_kernel(tc, x_crop, W_r, W_i, b_r, b_i, out):
             for u in group(c):
                 transposes(u)
                 h, w, t = units[u]
-                if (h, w) == (0, 1):
+                if (h, w) == (0, 0):
+                    load_x_half(1, t)
+                    if t == NBT // 2 - 1:
+                        load_w(2)
+                elif (h, w) == (0, 1):
                     load_x(1, t)
             for u in group(c):
                 copy_x(u, 0, "s")

@@ -23,7 +23,7 @@ W1_FIRST = 4
 W2_FIRST = 10
 W_DONE = 21
 LAG = 2
-W_LOAD_AFTER = 4
+W_LOAD_AFTER = 5
 
 
 def tile_dot_pa_t_kernel(tc, x_crop, W_r, W_i, b_r, b_i, out):
@@ -233,7 +233,7 @@ def tile_dot_pa_t_kernel(tc, x_crop, W_r, W_i, b_r, b_i, out):
                     nc.sync.dma_start(out=ovw[t, h, 1][:, ri, :], in_=piece)
                 return
             nc.scalar.activation(out=o[:, :, w, :], in_=o[:, :, w, :], func=RELU)
-            if h == 1 and t >= NBT - 1 - LAG:
+            if h == 1 and t >= NBT - 2 - LAG:
                 nc.sync.dma_start(out=ovw[t, h, w], in_=o[:, :, w, :])
             elif w == 1:
                 nc.sync.dma_start(out=ov[t, h], in_=o[:].rearrange("p r w f -> p r (w f)"))
@@ -268,7 +268,6 @@ def tile_dot_pa_t_kernel(tc, x_crop, W_r, W_i, b_r, b_i, out):
         nc.tensor.matmul(out=bps[:], lhsT=ones[:], rhs=brow[:], start=True, stop=True)
         for k in range(7):
             w_part(0, k)
-        nc.vector.tensor_copy(out=bias[:], in_=bps[:])
 
         starts = [sum(GROUPS[:j]) for j in range(len(GROUPS) + 1)]
         NG = len(GROUPS)
@@ -288,9 +287,11 @@ def tile_dot_pa_t_kernel(tc, x_crop, W_r, W_i, b_r, b_i, out):
                     load_x(1, t)
             for u in group(c):
                 copy_x(u, 0, "s")
-                copy_x(u, 1, "s" if c < W_DONE else "v")
+                copy_x(u, 1, "v" if W_DONE <= c < NU - 3 else "s")
             for u in group(c - 1):
                 quant_x(u)
+            if c == 2:
+                nc.vector.tensor_copy(out=bias[:], in_=bps[:])
             w_work(c)
             for u in group(c - 3):
                 add_bias(u)

from contextlib import ExitStack

import concourse.mybir as mybir
from concourse.masks import make_identity

F32 = mybir.dt.float32
BF16 = mybir.dt.bfloat16
U32 = mybir.dt.uint32
U8 = mybir.dt.uint8
FP8X4 = mybir.dt.float8_e4m3fn_x4
ADD = mybir.AluOpType.add
RELU = mybir.ActivationFunctionType.Relu

P = 128
B, C, F = 1024, 1024, 256
NBT = B // P
FLOPS = 4 * 4 * 2 * B * C * F

XBUFS = 8
OBUFS = 12
GROUPS = [1] * 32
W1_FIRST = 4
W2_FIRST = 10
W_DONE = 21
LAG = 2
W_LOAD_AFTER = 5


def tile_dot_pa_t_kernel(tc, x_crop, W_r, W_i, b_r, b_i, out):
    nc = tc.nc
    xv = x_crop.rearrange("(t b) r h w c -> t h b r (w c)", b=P)
    xvw = x_crop.rearrange("(t b) r h w c -> t h w b r c", b=P)
    ov = out.rearrange("(t b) r h w f -> t h b r (w f)", b=P)
    ovw = out.rearrange("(t b) r h w f -> t h w b r f", b=P)
    wv = {
        "r": W_r.rearrange("h w (s p e) f -> h w p s (e f)", s=4, p=P, e=2),
        "i": W_i.rearrange("h w (s p e) f -> h w p s (e f)", s=4, p=P, e=2),
    }
    units = [(0, w, t) for w in range(2) for t in range(NBT)]
    for i in range(NBT + LAG):
        if i < NBT:
            units.append((1, 0, i))
        if i >= LAG:
            units.append((1, 1, i - LAG))
    NU = len(units)

    with ExitStack() as ctx:
        const = ctx.enter_context(tc.tile_pool(name="const", bufs=1))
        xpool = ctx.enter_context(tc.tile_pool(name="xraw", bufs=XBUFS))
        wrawp = ctx.enter_context(tc.tile_pool(name="wraw", bufs=4))
        gwp = ctx.enter_context(tc.tile_pool(name="gw", bufs=2))
        gxp = ctx.enter_context(tc.tile_pool(name="gx", bufs=4))
        xcp = ctx.enter_context(tc.tile_pool(name="xc", bufs=6))
        otp = ctx.enter_context(tc.tile_pool(name="ot", bufs=OBUFS))
        pst = ctx.enter_context(tc.psum_pool(name="pst", bufs=4))
        psa = ctx.enter_context(tc.psum_pool(name="psa", bufs=4))
        ctx.enter_context(tc.manual_schedule())

        wc = const.tile([P, 4 * 1536], U32, align_bytes=64)
        ws = const.tile([P, 4 * 1536], U8, align_bytes=64)
        ident = const.tile([P, P], F32)
        ones = const.tile([P, P], BF16)
        brow = const.tile([P, 2 * F], BF16)
        bias = const.tile([P, 2 * F], F32)
        warm = const.tile([P, 1], F32)

        xraw = {}
        xhalf = {}
        wraw = {}
        gws = {}
        gxs = {}
        xcs = {}
        xss = {}
        accs = {}
        ots = {}
        banks = {}
        w_ready = []

        def load_w(px):
            for m in ("i", "r"):
                t = wrawp.tile([P, 2048], BF16, name="wraw")
                nc.sync.dma_start(
                    out=t[:].rearrange("p (s k) -> p s k", s=4), in_=wv[m][px // 2, px % 2]
                )
                wraw[(px, m)] = t

        def load_x_half(w, t):
            xhalf[(w, t)] = xpool.tile([P, 4096], BF16, name="xraw")
            nc.sync.dma_start(
                out=xhalf[(w, t)][:, 0:2048].rearrange("p (r c) -> p r c", r=2), in_=xvw[t, 0, w]
            )

        def load_x(h, t):
            xraw[(h, t)] = xpool.tile([P, 4096], BF16, name="xraw")
            nc.sync.dma_start(
                out=xraw[(h, t)][:].rearrange("p (r k) -> p r k", r=2), in_=xv[t, h]
            )

        def regroup_w(px, m, g, eng="v"):
            if px not in gws:
                gws[px] = gwp.tile([P, 6144], BF16, name="gw", align_bytes=64)
            col0 = 256 if m == "r" else 512
            src = wraw[(px, m)][:, g * 1024 : (g + 1) * 1024].rearrange(
                "p (t c i) -> p c t i", t=4, i=4
            )
            lo = g * 3072 + col0 * 4
            dst = gws[px][:, lo : lo + 1024].rearrange("p (c i t) -> p c t i", i=4, t=4)
            if eng == "v":
                nc.vector.tensor_copy(out=dst, in_=src)
            else:
                nc.scalar.copy(out=dst, in_=src)

        def negate_w(px):
            g3 = gws[px][:].rearrange("p (g m) -> p g m", g=2)
            nc.vector.tensor_scalar_mul(out=g3[:, :, 0:1024], in0=g3[:, :, 2048:3072], scalar1=-1.0)

        def quant_w(px, j):
            wlo = px * 1536 + j * 512
            nc.vector.quantize_mx(
                out=wc[:, wlo : wlo + 512].bitcast(FP8X4),
                scales=ws[:, wlo : wlo + 512],
                in_=gws[px][:, j * 2048 : (j + 1) * 2048],
            )

        def w_part(px, k):
            if k == 0:
                regroup_w(px, "i", 0)
            elif k == 1:
                regroup_w(px, "i", 1)
            elif k == 2:
                negate_w(px)
            elif k == 3:
                regroup_w(px, "r", 0)
                regroup_w(px, "r", 1, "s")
                if px == 1:
                    load_w(3)
            else:
                quant_w(px, (1, 0, 2)[k - 4])
                if k == 6:
                    w_ready.append(px)

        w_plan = {}
        for k in range(7):
            w_plan.setdefault(W1_FIRST + (6 * k) // 7, []).append((1, k))
        for k in range(14):
            w_plan.setdefault(W2_FIRST + (11 * k) // 14, []).append((2 + k // 7, k % 7))

        def w_work(c):
            for px, k in w_plan.get(c, []):
                w_part(px, k)

        def transposes(u):
            h, w, t = units[u]
            xw = (xhalf[(w, t)][:, 0:2048] if h == 0 else xraw[(h, t)][:]).bitcast(F32)
            banks[u] = []
            for ri in range(2):
                off = ri * 512 if h == 0 else (ri * 2 + w) * 512
                xt = pst.tile([P, 4, P], F32, name="xt")
                for j in range(4):
                    nc.tensor.transpose(xt[:, j, :], xw[:, off + j * P : off + (j + 1) * P], ident[:])
                banks[u].append(xt)

        def copy_x(u, ri, eng):
            if ri == 0:
                gxs[u] = gxp.tile([P, 2048], BF16, name="gx", align_bytes=64)
            dst = gxs[u][:].bitcast(F32)[:, ri * 512 : (ri + 1) * 512].rearrange(
                "p (g b u) -> p g b u", g=2, b=P, u=2
            )
            src = banks[u][ri][:].rearrange("p (g u) b -> p g b u", g=2, u=2)
            if eng == "v":
                nc.vector.tensor_copy(out=dst, in_=src)
            else:
                nc.scalar.copy(out=dst, in_=src)

        def quant_x(u):
            xcs[u] = xcp.tile([P, 512], U32, name="xc", align_bytes=64)
            xss[u] = xcp.tile([P, 512], U8, name="xs", align_bytes=64)
            nc.vector.quantize_mx(out=xcs[u][:].bitcast(FP8X4), scales=xss[u][:], in_=gxs[u][:])

        def mx_group(u, acc, c0, n):
            h, w, t = units[u]
            px = 2 * h + w
            assert px in w_ready
            k = 0
            for ri in range(2):
                for g in range(2):
                    lo = ri * 256 + g * P
                    wlo = px * 1536 + g * 768 + (256 if ri == 0 else 0) + c0
                    nc.tensor.matmul_mx(
                        out=acc,
                        lhsT=xcs[u][:, lo : lo + P].bitcast(FP8X4),
                        lhsT_scale=xss[u][:, lo : lo + P],
                        rhs=wc[:, wlo : wlo + n].bitcast(FP8X4),
                        rhs_scale=ws[:, wlo : wlo + n],
                        start=(k == 0),
                        stop=(k == 3),
                    )
                    k += 1

        def mx_unit(u):
            if u == NU - 1:
                for ri in range(2):
                    accs[(u, ri)] = psa.tile([P, F], F32, name="acc")
                    mx_group(u, accs[(u, ri)][:], ri * F, F)
            else:
                accs[u] = psa.tile([P, 512], F32, name="acc")
                mx_group(u, accs[u][:], 0, 512)

        def add_bias(u):
            h, w, t = units[u]
            if w == 0:
                ots[(h, t)] = otp.tile([P, 2, 2, F], F32, name="ot")
            o = ots[(h, t)]
            if u == NU - 1:
                return
            nc.vector.tensor_tensor(
                out=o[:, :, w, :],
                in0=accs[u][:].rearrange("p (r f) -> p r f", r=2),
                in1=bias[:].rearrange("p (r f) -> p r f", r=2),
                op=ADD,
            )

        def relu_store(u):
            h, w, t = units[u]
            o = ots[(h, t)]
            if u == NU - 1:
                for ri in range(2):
                    piece = o[:, ri, 1, :]
                    nc.vector.tensor_tensor(
                        out=piece, in0=accs[(u, ri)][:], in1=bias[:, ri * F : (ri + 1) * F], op=ADD
                    )
                    nc.scalar.activation(out=piece, in_=piece, func=RELU)
                    nc.sync.dma_start(out=ovw[t, h, 1][:, ri, :], in_=piece)
                return
            nc.scalar.activation(out=o[:, :, w, :], in_=o[:, :, w, :], func=RELU)
            if h == 1 and t >= NBT - 2 - LAG:
                nc.sync.dma_start(out=ovw[t, h, w], in_=o[:, :, w, :])
            elif w == 1:
                nc.sync.dma_start(out=ov[t, h], in_=o[:].rearrange("p r w f -> p r (w f)"))

        def keep_clock(px, m, n):
            for j in range(n):
                nc.tensor.matmul(
                    out=spare[:],
                    lhsT=ones[:],
                    rhs=wraw[(px, m)][:, (j % 4) * 512 : (j % 4 + 1) * 512],
                    start=True,
                    stop=True,
                )

        make_identity(nc, ident[:])
        nc.vector.memset(ones[:], 1.0)
        nc.vector.memset(brow[:], 0.0)
        nc.scalar.dma_start(out=brow[0:1, 0:F], in_=b_r.rearrange("(o f) -> o f", o=1))
        nc.scalar.dma_start(out=brow[0:1, F : 2 * F], in_=b_i.rearrange("(o f) -> o f", o=1))
        nc.scalar.activation(out=warm[:], in_=ones[:, 0:1], func=RELU)

        load_w(0)
        for t in range(NBT):
            if t == W_LOAD_AFTER:
                load_w(1)
            load_x_half(0, t)

        spare = psa.tile([P, 512], F32, name="acc")
        keep_clock(0, "i", 3)
        keep_clock(0, "r", 4)
        bps = psa.tile([P, 512], F32, name="acc")
        nc.tensor.matmul(out=bps[:], lhsT=ones[:], rhs=brow[:], start=True, stop=True)
        for k in range(7):
            w_part(0, k)

        starts = [sum(GROUPS[:j]) for j in range(len(GROUPS) + 1)]
        NG = len(GROUPS)

        def group(j):
            return list(range(starts[j], starts[j + 1])) if 0 <= j < NG else []

        for c in range(NG + 4):
            for u in group(c):
                transposes(u)
                h, w, t = units[u]
                if (h, w) == (0, 0):
                    load_x_half(1, t)
                    if t == NBT // 2 - 1:
                        load_w(2)
                elif (h, w) == (0, 1):
                    load_x(1, t)
            for u in group(c):
                copy_x(u, 0, "s")
                copy_x(u, 1, "v" if W_DONE <= c < NU - 3 else "s")
            for u in group(c - 1):
                quant_x(u)
            if c == 2:
                nc.vector.tensor_copy(out=bias[:], in_=bps[:])
            w_work(c)
            for u in group(c - 3):
                add_bias(u)
            for u in group(c - 4):
                if u < NU - 1:
                    relu_store(u)
            if c - 3 == NU - 1:
                relu_store(NU - 1)
            for u in group(c - 2):
                mx_unit(u)
